import numpy as np
import ml_dtypes


def mxq(x, axis, fmt="e4m3"):
    dtype, down = {"e4m3": (ml_dtypes.float8_e4m3fn, 7), "e5m2": (ml_dtypes.float8_e5m2, 14)}[fmt]
    v = np.moveaxis(np.asarray(x, np.float32).astype(ml_dtypes.bfloat16).astype(np.float64), axis, -1)
    blocks = v.reshape(v.shape[:-1] + (-1, 32))
    amax = np.abs(blocks).max(-1, keepdims=True)
    byte = np.maximum(np.where(amax > 0, np.frexp(amax)[1] - 1 + 127, 0) - down, 1)
    scale = np.exp2(byte - 127.0)
    codes = (blocks / scale).astype(np.float32).astype(dtype).astype(np.float64)
    return np.moveaxis((codes * scale).reshape(v.shape), -1, axis)


WIDE = False


def mx_kscale(k):
    if not WIDE:
        return np.ones(k)
    levels = np.array([10, -10, 5, -5, 0])
    if k % 512:
        return np.exp2(np.random.permutation(np.resize(levels, k // 32))).repeat(32)
    a = np.empty((k // 512, 16))
    for p in range(k // 512):
        a[p, :8] = np.random.permutation(np.resize(levels, 8))
        for g in range(8):
            far = levels[np.abs(levels - a[p, g]) >= 10]
            a[p, g + 8] = far[np.random.randint(len(far))]
    return np.exp2(a.ravel()).repeat(32)


BF16 = ml_dtypes.bfloat16


def bf(x):
    return np.asarray(x, np.float32).astype(BF16)


def f64(x):
    return np.asarray(x).astype(np.float64)


B, CK, CV, NO, T, H, W = 16, 128, 256, 2, 2, 16, 16
N = T * H * W
P = H * W
C = NO * CV


def setup_inputs():
    s = mx_kscale(N)
    g = np.exp2(np.round(np.log2(np.mean(s))))
    mk = np.random.standard_normal((B, CK, N))
    qk = np.random.standard_normal((B, CK, P))
    qe = np.random.uniform(0.0, 1.0, (B, CK, P))
    ms = bf(0.75 + 0.5 * np.random.uniform(0.0, 1.0, (B, N)))
    d = (np.log2(np.max(s)) - np.log2(s))[None, :] * np.log(2.0) * np.sqrt(CK) / f64(ms)
    a0 = mk[:, 0, :] ** 2 + d
    mk[:, 0, :] = np.sqrt(a0)
    qk[:, 0, :] = 0.0
    qe[:, 0, :] = 1.0
    mk, qk, qe = bf(mk), bf(qk), bf(qe)
    mksq = f64(mk) * f64(mk)
    mksq[:, 0, :] = a0
    return {"memory_key": mk,
            "memory_key_sq": bf(mksq),
            "query_key": qk,
            "query_selection": qe,
            "query_key_sel": bf(f64(qk) * f64(qe)),
            "memory_shrinkage": ms,
            "memory_value": bf(np.random.standard_normal((B, C, N)) * g / s[None, None, :])}


def reference(memory_key, memory_key_sq, query_key, query_selection, query_key_sel, memory_shrinkage, memory_value):
    qe = f64(query_selection)
    qs = f64(query_key_sel)
    ms = f64(memory_shrinkage)[:, :, None]
    a_sq = f64(memory_key_sq).transpose(0, 2, 1) @ qe
    two_ab = 2.0 * (f64(memory_key).transpose(0, 2, 1) @ qs)
    b_sq = np.sum(qs * f64(query_key), axis=1, keepdims=True)
    similarity = (-a_sq + two_ab - b_sq) * ms * (1.0 / np.sqrt(CK))
    e = np.exp(similarity - similarity.max(axis=1, keepdims=True))
    affinity = e / e.sum(axis=1, keepdims=True)
    return mxq(f64(memory_value), 2, "e4m3") @ mxq(affinity, 1, "e4m3")

@@ -1,0 +1,329 @@
+import math
+from contextlib import ExitStack
+
+import concourse.mybir as mybir
+from concourse.masks import make_identity
+
+F32 = mybir.dt.float32
+BF16 = mybir.dt.bfloat16
+U32 = mybir.dt.uint32
+U8 = mybir.dt.uint8
+FP8X4 = mybir.dt.float8_e4m3fn_x4
+ALU = mybir.AluOpType
+ACT = mybir.ActivationFunctionType
+AXIS = mybir.AxisListType
+
+P = 128
+B = 16
+N = 512
+Q = 256
+C = 512
+Q_TILES = Q // P
+C_TILES = C // P
+PACK = 4
+INV_SQRT_CK = 1.0 / math.sqrt(128.0)
+LOAD_AHEAD = 4
+
+FLOPS = B * (2 * 2 * P * N * Q + 2 * C * N * Q)
+
+
+def tile_vidsam_pa_t_kernel(
+    tc,
+    memory_key,
+    memory_key_sq,
+    query_key,
+    query_selection,
+    query_key_sel,
+    memory_shrinkage,
+    memory_value,
+    out,
+):
+    nc = tc.nc
+    with ExitStack() as ctx:
+        consts = ctx.enter_context(tc.tile_pool(name="consts", bufs=1))
+        loads = ctx.enter_context(tc.tile_pool(name="loads", bufs=B))
+        work = ctx.enter_context(tc.tile_pool(name="work", bufs=3))
+        psum = ctx.enter_context(tc.psum_pool(name="psum", bufs=8))
+        ctx.enter_context(tc.manual_schedule())
+
+        ms_rows = consts.tile([P, N], BF16)
+        nc.vector.memset(ms_rows[:], 0.0)
+        nc.sync.dma_start(out=ms_rows[0:B, :], in_=memory_shrinkage)
+        qe_sb, ksq_sb, qs_sb, key_sb, qk_sb, val_sb = {}, {}, {}, {}, {}, {}
+
+        def load(b):
+            qs_sb[b] = loads.tile([P, Q], BF16, name="qs")
+            nc.sync.dma_start(out=qs_sb[b][:], in_=query_key_sel[b])
+            qk_sb[b] = loads.tile([P, Q], BF16, name="qk")
+            nc.sync.dma_start(out=qk_sb[b][:], in_=query_key[b])
+            qe_sb[b] = loads.tile([P, Q], BF16, name="qe")
+            nc.sync.dma_start(out=qe_sb[b][:], in_=query_selection[b])
+            ksq_sb[b] = loads.tile([P, N], BF16, name="ksq")
+            nc.sync.dma_start(out=ksq_sb[b][:], in_=memory_key_sq[b])
+            key_sb[b] = loads.tile([P, N], BF16, name="key")
+            nc.sync.dma_start(out=key_sb[b][:], in_=memory_key[b])
+            val_sb[b] = loads.tile([P, C_TILES * N], BF16, name="val")
+            nc.sync.dma_start(
+                out=val_sb[b][:],
+                in_=memory_value[b].rearrange("(r t) n -> r (t n)", t=C_TILES),
+            )
+
+        for b in range(LOAD_AHEAD):
+            load(b)
+
+        ident_bf = consts.tile([P, P], BF16)
+        make_identity(nc, ident_bf[:])
+        ident_f32 = consts.tile([P, P], F32)
+        make_identity(nc, ident_f32[:])
+        ones_f32 = consts.tile([P, 2], F32)
+        nc.vector.memset(ones_f32[:], 1.0)
+        warm = consts.tile([P, 1], F32)
+        nc.scalar.activation(out=warm[:], in_=ones_f32[:, 0:1], func=ACT.Exp)
+
+        ms_rows_ew = ms_rows[:].rearrange("r (q u e) -> r e u q", u=2, e=2)
+        ms_cols_ps = psum.tile([P, 4, P], BF16, tag="bank")
+        for e in range(2):
+            for u in range(2):
+                nc.tensor.transpose(
+                    ms_cols_ps[:, 2 * e + u, :],
+                    ms_rows_ew[:, e, u, :],
+                    ident_bf[:],
+                )
+        ms_cols = consts.tile([P, 4, B], BF16)
+        nc.vector.tensor_copy(out=ms_cols[:], in_=ms_cols_ps[:, :, 0:B])
+
+        qs_m2, prod = {}, {}
+        shrink = consts.tile([P, B, N], BF16)
+        bsq_ps, d_ps, dist, dist_min, neg_max = {}, {}, {}, {}, {}
+        expo, expo_sum, inv_sum = {}, {}, {}
+        affinity, aff_flipped, aff_grouped, aff_codes, aff_scales = {}, {}, {}, {}, {}
+        val_grouped, val_codes, val_scales = {}, {}, {}
+        o_ps, result = {}, {}
+
+        def prepare_queries(b):
+            qs_m2[b] = work.tile([P, Q], BF16, name="qs_m2", bufs=3)
+            nc.gpsimd.tensor_scalar(
+                out=qs_m2[b][:], in0=qs_sb[b][:], scalar1=-2.0, scalar2=0.0, op0=ALU.mult, op1=ALU.add
+            )
+            prod[b] = work.tile([P, Q], F32, name="prod", bufs=3)
+            nc.gpsimd.tensor_tensor(out=prod[b][:], in0=qs_sb[b][:], in1=qk_sb[b][:], op=ALU.mult)
+
+        def spread_shrinkage(b):
+            spread_ps = psum.tile([P, 2, N], BF16, tag="bank")
+            for j in range(2):
+                for k in range(4):
+                    nc.tensor.transpose(
+                        spread_ps[:, j, k * P : (k + 1) * P],
+                        ms_cols[:, k, b + j : b + j + 1].to_broadcast([P, P]),
+                        ident_bf[:],
+                    )
+            nc.scalar.copy(out=shrink[:, b : b + 2, :], in_=spread_ps[:])
+
+        def distances(b):
+            for i in range(Q_TILES):
+                q_cols = slice(i * P, (i + 1) * P)
+                d_ps[b, i] = psum.tile([P, 2, 2, P], F32, tag="bank", name="d_ps")
+                nc.tensor.matmul(
+                    out=d_ps[b, i][:],
+                    lhsT=qe_sb[b][:, q_cols],
+                    rhs=ksq_sb[b][:].rearrange("c (q u e) -> c e u q", u=2, e=2),
+                    start=True,
+                    stop=False,
+                )
+                nc.tensor.matmul(
+                    out=d_ps[b, i][:],
+                    lhsT=qs_m2[b][:, q_cols],
+                    rhs=key_sb[b][:].rearrange("c (q u e) -> c e u q", u=2, e=2),
+                    start=False,
+                    stop=True,
+                )
+            bsq_ps[b] = psum.tile([P, Q_TILES, 2], F32, tag="bank", name="bsq_ps")
+            for i in range(Q_TILES):
+                nc.tensor.matmul(
+                    out=bsq_ps[b][:, i, :],
+                    lhsT=prod[b][:, i * P : (i + 1) * P],
+                    rhs=ones_f32[:],
+                    start=True,
+                    stop=True,
+                )
+
+        def scale_distances(b, i):
+            if i == 0:
+                dist[b] = work.tile([P, Q_TILES, N], F32, name="dist")
+            nc.vector.scalar_tensor_tensor(
+                out=dist[b][:, i, :],
+                in0=d_ps[b, i][:].rearrange("p e u q -> p (e u q)"),
+                scalar=bsq_ps[b][:, i, 0:1],
+                in1=shrink[:, b, :],
+                op0=ALU.add,
+                op1=ALU.mult,
+            )
+
+        def row_minimum(b, i):
+            if i == 0:
+                dist_min[b] = work.tile([P, Q_TILES], F32, name="dist_min")
+            nc.vector.tensor_reduce(
+                out=dist_min[b][:, i : i + 1], in_=dist[b][:, i, :], axis=AXIS.X, op=ALU.min
+            )
+
+        def negated_maximum(b):
+            neg_max[b] = work.tile([P, Q_TILES], F32, name="neg_max")
+            nc.vector.tensor_scalar(
+                out=neg_max[b][:], in0=dist_min[b][:], scalar1=INV_SQRT_CK, scalar2=None, op0=ALU.mult
+            )
+
+        def exponentials(b):
+            expo[b] = work.tile([P, Q_TILES, N], F32, name="expo")
+            expo_sum[b] = work.tile([P, Q_TILES], F32, name="expo_sum")
+            for i in range(Q_TILES):
+                nc.scalar.activation(
+                    out=expo[b][:, i, :],
+                    in_=dist[b][:, i, :],
+                    func=ACT.Exp,
+                    bias=neg_max[b][:, i : i + 1],
+                    scale=-INV_SQRT_CK,
+                    accum_out=expo_sum[b][:, i : i + 1],
+                )
+
+        def invert_sums(b):
+            inv_sum[b] = work.tile([P, Q_TILES], F32, name="inv_sum")
+            nc.vector.reciprocal(out=inv_sum[b][:], in_=expo_sum[b][:])
+
+        def normalise(b):
+            affinity[b] = work.tile([P, Q_TILES, N], BF16, name="affinity", bufs=2)
+            for i in range(Q_TILES):
+                nc.gpsimd.tensor_scalar(
+                    out=affinity[b][:, i, :],
+                    in0=expo[b][:, i, :],
+                    scalar1=inv_sum[b][:, i : i + 1],
+                    scalar2=0.0,
+                    op0=ALU.mult,
+                    op1=ALU.add,
+                )
+
+        def transpose_affinity(b):
+            aff_flipped[b] = psum.tile([P, PACK, Q], BF16, tag="bank", name="aff_flipped")
+            for i in range(Q_TILES):
+                for e in range(2):
+                    for u in range(2):
+                        first = (2 * e + u) * P
+                        nc.tensor.transpose(
+                            aff_flipped[b][:, 2 * u + e, i * P : (i + 1) * P],
+                            affinity[b][:, i, first : first + P],
+                            ident_bf[:],
+                        )
+
+        def group_affinity(b):
+            aff_grouped[b] = work.tile([P, Q, PACK], BF16, align_bytes=64, name="aff_grouped", bufs=2)
+            nc.scalar.copy(out=aff_grouped[b][:], in_=aff_flipped[b][:].rearrange("q k p -> q p k"))
+
+        def quantise_affinity(b):
+            aff_codes[b] = work.tile([P, Q], U32, align_bytes=64, name="aff_codes")
+            aff_scales[b] = work.tile([P, Q], U8, align_bytes=64, name="aff_scales")
+            nc.vector.quantize_mx(
+                out=aff_codes[b][:].bitcast(FP8X4),
+                scales=aff_scales[b][:],
+                in_=aff_grouped[b][:].rearrange("q p k -> q (p k)"),
+            )
+
+        def transpose_values(b):
+            val_words = val_sb[b][:].bitcast(F32)
+            val_grouped[b] = work.tile([P, C * PACK], BF16, align_bytes=64, name="val_grouped", bufs=2)
+            grouped_words = val_grouped[b][:].bitcast(F32)
+            for h in range(2):
+                flipped = psum.tile([P, 2, 2 * P], F32, tag="bank")
+                for tl in range(2):
+                    for u in range(2):
+                        first = (2 * h + tl) * (N // 2)
+                        nc.tensor.transpose(
+                            flipped[:, u, tl * P : (tl + 1) * P],
+                            val_words[:, first + u : first + N // 2 : 2],
+                            ident_f32[:],
+                        )
+                nc.scalar.copy(
+                    out=grouped_words[:, h * N : (h + 1) * N].rearrange("q (c u) -> q c u", u=2),
+                    in_=flipped[:].rearrange("q u c -> q c u"),
+                )
+
+        def quantise_values(b):
+            val_codes[b] = work.tile([P, C], U32, align_bytes=64, name="val_codes")
+            val_scales[b] = work.tile([P, C], U8, align_bytes=64, name="val_scales")
+            nc.vector.quantize_mx(
+                out=val_codes[b][:].bitcast(FP8X4), scales=val_scales[b][:], in_=val_grouped[b][:]
+            )
+
+        def read_memory(b):
+            for h in range(2):
+                o_ps[b, h] = psum.tile([P, 2, Q], F32, tag="bank", name="o_ps")
+                for tl in range(2):
+                    c_cols = slice((2 * h + tl) * P, (2 * h + tl + 1) * P)
+                    nc.tensor.matmul_mx(
+                        out=o_ps[b, h][:, tl, :],
+                        lhsT=val_codes[b][:, c_cols].bitcast(FP8X4),
+                        lhsT_scale=val_scales[b][:, c_cols],
+                        rhs=aff_codes[b][:].bitcast(FP8X4),
+                        rhs_scale=aff_scales[b][:],
+                        start=True,
+                        stop=True,
+                    )
+
+        def copy_result_vector(b):
+            result[b] = work.tile([P, C_TILES * Q], F32, name="result")
+            nc.vector.tensor_copy(
+                out=result[b][:, 2 * Q : 4 * Q], in_=o_ps[b, 1][:].rearrange("r t p -> r (t p)")
+            )
+
+        def copy_result_scalar(b):
+            nc.scalar.copy(out=result[b][:, 0 : 2 * Q], in_=o_ps[b, 0][:].rearrange("r t p -> r (t p)"))
+
+        def store_result(b, h):
+            half = slice(h * 2 * Q, (h + 1) * 2 * Q)
+            nc.sync.dma_start(
+                out=out[b].rearrange("(r t) p -> r (t p)", t=C_TILES)[:, half], in_=result[b][:, half]
+            )
+
+        def live(b):
+            return 0 <= b < B
+
+        prepare_queries(0)
+        for step in range(-1, B + 4):
+            if live(step + LOAD_AHEAD + 1):
+                load(step + LOAD_AHEAD + 1)
+            if live(step - 1):
+                exponentials(step - 1)
+            if live(step - 3):
+                group_affinity(step - 3)
+            if live(step - 2):
+                transpose_values(step - 2)
+            if live(step - 4):
+                read_memory(step - 4)
+            if live(step):
+                scale_distances(step, 0)
+                scale_distances(step, 1)
+                row_minimum(step, 0)
+                row_minimum(step, 1)
+            if live(step - 2):
+                normalise(step - 2)
+            if live(step + 2):
+                prepare_queries(step + 2)
+            if live(step - 4):
+                copy_result_vector(step - 4)
+                store_result(step - 4, 1)
+            if live(step):
+                negated_maximum(step)
+            if live(step - 3):
+                quantise_values(step - 3)
+                quantise_affinity(step - 3)
+            if live(step - 1):
+                invert_sums(step - 1)
+            if live(4 * (step + 1)):
+                spread_shrinkage(4 * (step + 1))
+            if live(step - 4):
+                copy_result_scalar(step - 4)
+                store_result(step - 4, 0)
+            if live(step + 1):
+                distances(step + 1)
+            if live(4 * (step + 1)):
+                spread_shrinkage(4 * (step + 1) + 2)
+            if live(step - 2):
+                transpose_affinity(step - 2)

@@ -80,15 +80,9 @@ def tile_vidsam_pa_t_kernel(
         warm = consts.tile([P, 1], F32)
         nc.scalar.activation(out=warm[:], in_=ones_f32[:, 0:1], func=ACT.Exp)
 
-        ms_rows_ew = ms_rows[:].rearrange("r (q u e) -> r e u q", u=2, e=2)
         ms_cols_ps = psum.tile([P, 4, P], BF16, tag="bank")
-        for e in range(2):
-            for u in range(2):
-                nc.tensor.transpose(
-                    ms_cols_ps[:, 2 * e + u, :],
-                    ms_rows_ew[:, e, u, :],
-                    ident_bf[:],
-                )
+        for k in range(4):
+            nc.tensor.transpose(ms_cols_ps[:, k, :], ms_rows[:, k * P : (k + 1) * P], ident_bf[:])
         ms_cols = consts.tile([P, 4, B], BF16)
         nc.vector.tensor_copy(out=ms_cols[:], in_=ms_cols_ps[:, :, 0:B])
 
@@ -122,18 +116,18 @@ def tile_vidsam_pa_t_kernel(
         def distances(b):
             for i in range(Q_TILES):
                 q_cols = slice(i * P, (i + 1) * P)
-                d_ps[b, i] = psum.tile([P, 2, 2, P], F32, tag="bank", name="d_ps")
+                d_ps[b, i] = psum.tile([P, N], F32, tag="bank", name="d_ps")
                 nc.tensor.matmul(
                     out=d_ps[b, i][:],
                     lhsT=qe_sb[b][:, q_cols],
-                    rhs=ksq_sb[b][:].rearrange("c (q u e) -> c e u q", u=2, e=2),
+                    rhs=ksq_sb[b][:],
                     start=True,
                     stop=False,
                 )
                 nc.tensor.matmul(
                     out=d_ps[b, i][:],
                     lhsT=qs_m2[b][:, q_cols],
-                    rhs=key_sb[b][:].rearrange("c (q u e) -> c e u q", u=2, e=2),
+                    rhs=key_sb[b][:],
                     start=False,
                     stop=True,
                 )
@@ -152,7 +146,7 @@ def tile_vidsam_pa_t_kernel(
                 dist[b] = work.tile([P, Q_TILES, N], F32, name="dist")
             nc.vector.scalar_tensor_tensor(
                 out=dist[b][:, i, :],
-                in0=d_ps[b, i][:].rearrange("p e u q -> p (e u q)"),
+                in0=d_ps[b, i][:],
                 scalar=bsq_ps[b][:, i, 0:1],
                 in1=shrink[:, b, :],
                 op0=ALU.add,
@@ -193,8 +187,8 @@ def tile_vidsam_pa_t_kernel(
             affinity[b] = work.tile([P, Q_TILES, N], BF16, name="affinity", bufs=2)
             for i in range(Q_TILES):
                 nc.gpsimd.tensor_scalar(
-                    out=affinity[b][:, i, :],
-                    in0=expo[b][:, i, :],
+                    out=affinity[b][:, i, :].rearrange("p (u q e) -> p u q e", u=2, e=2),
+                    in0=expo[b][:, i, :].rearrange("p (q u e) -> p u q e", u=2, e=2),
                     scalar1=inv_sum[b][:, i : i + 1],
                     scalar2=0.0,
                     op0=ALU.mult,
@@ -202,20 +196,22 @@ def tile_vidsam_pa_t_kernel(
                 )
 
         def transpose_affinity(b):
-            aff_flipped[b] = psum.tile([P, PACK, Q], BF16, tag="bank", name="aff_flipped")
+            aff_flipped[b] = psum.tile([P, 2, Q], F32, tag="bank", name="aff_flipped")
             for i in range(Q_TILES):
-                for e in range(2):
-                    for u in range(2):
-                        first = (2 * e + u) * P
-                        nc.tensor.transpose(
-                            aff_flipped[b][:, 2 * u + e, i * P : (i + 1) * P],
-                            affinity[b][:, i, first : first + P],
-                            ident_bf[:],
-                        )
+                aff_words = affinity[b][:, i, :].bitcast(F32)
+                for u in range(2):
+                    nc.tensor.transpose(
+                        aff_flipped[b][:, u, i * P : (i + 1) * P],
+                        aff_words[:, u * P : (u + 1) * P],
+                        ident_f32[:],
+                    )
 
         def group_affinity(b):
             aff_grouped[b] = work.tile([P, Q, PACK], BF16, align_bytes=64, name="aff_grouped", bufs=2)
-            nc.scalar.copy(out=aff_grouped[b][:], in_=aff_flipped[b][:].rearrange("q k p -> q p k"))
+            nc.scalar.copy(
+                out=aff_grouped[b][:].bitcast(F32),
+                in_=aff_flipped[b][:].rearrange("q u p -> q p u"),
+            )
 
         def quantise_affinity(b):
             aff_codes[b] = work.tile([P, Q], U32, align_bytes=64, name="aff_codes")

@@ -71,8 +71,6 @@ def tile_vidsam_pa_t_kernel(
         for b in range(LOAD_AHEAD):
             load(b)
 
-        ident_bf = consts.tile([P, P], BF16)
-        make_identity(nc, ident_bf[:])
         ident_f32 = consts.tile([P, P], F32)
         make_identity(nc, ident_f32[:])
         ones_f32 = consts.tile([P, 2], F32)
@@ -80,10 +78,11 @@ def tile_vidsam_pa_t_kernel(
         warm = consts.tile([P, 1], F32)
         nc.scalar.activation(out=warm[:], in_=ones_f32[:, 0:1], func=ACT.Exp)
 
-        ms_cols_ps = psum.tile([P, 4, P], BF16, tag="bank")
-        for k in range(4):
-            nc.tensor.transpose(ms_cols_ps[:, k, :], ms_rows[:, k * P : (k + 1) * P], ident_bf[:])
-        ms_cols = consts.tile([P, 4, B], BF16)
+        ms_words = ms_rows[:].bitcast(F32)
+        ms_cols_ps = psum.tile([P, 2, P], F32, tag="bank")
+        for k in range(2):
+            nc.tensor.transpose(ms_cols_ps[:, k, :], ms_words[:, k * P : (k + 1) * P], ident_f32[:])
+        ms_cols = consts.tile([P, 2, B], F32)
         nc.vector.tensor_copy(out=ms_cols[:], in_=ms_cols_ps[:, :, 0:B])
 
         qs_m2, prod = {}, {}
@@ -103,34 +102,27 @@ def tile_vidsam_pa_t_kernel(
             nc.gpsimd.tensor_tensor(out=prod[b][:], in0=qs_sb[b][:], in1=qk_sb[b][:], op=ALU.mult)
 
         def spread_shrinkage(b):
-            spread_ps = psum.tile([P, 2, N], BF16, tag="bank")
+            spread_ps = psum.tile([P, 2, N // 2], F32, tag="bank")
             for j in range(2):
-                for k in range(4):
+                for k in range(2):
                     nc.tensor.transpose(
                         spread_ps[:, j, k * P : (k + 1) * P],
                         ms_cols[:, k, b + j : b + j + 1].to_broadcast([P, P]),
-                        ident_bf[:],
+                        ident_f32[:],
                     )
-            nc.scalar.copy(out=shrink[:, b : b + 2, :], in_=spread_ps[:])
+            nc.scalar.copy(out=shrink[:, b : b + 2, :].bitcast(F32), in_=spread_ps[:])
 
-        def distances(b):
-            for i in range(Q_TILES):
-                q_cols = slice(i * P, (i + 1) * P)
-                d_ps[b, i] = psum.tile([P, N], F32, tag="bank", name="d_ps")
-                nc.tensor.matmul(
-                    out=d_ps[b, i][:],
-                    lhsT=qe_sb[b][:, q_cols],
-                    rhs=ksq_sb[b][:],
-                    start=True,
-                    stop=False,
-                )
-                nc.tensor.matmul(
-                    out=d_ps[b, i][:],
-                    lhsT=qs_m2[b][:, q_cols],
-                    rhs=key_sb[b][:],
-                    start=False,
-                    stop=True,
-                )
+        def distances(b, i):
+            q_cols = slice(i * P, (i + 1) * P)
+            d_ps[b, i] = psum.tile([P, N], F32, tag="bank", name="d_ps")
+            nc.tensor.matmul(
+                out=d_ps[b, i][:], lhsT=qe_sb[b][:, q_cols], rhs=ksq_sb[b][:], start=True, stop=False
+            )
+            nc.tensor.matmul(
+                out=d_ps[b, i][:], lhsT=qs_m2[b][:, q_cols], rhs=key_sb[b][:], start=False, stop=True
+            )
+
+        def query_squares(b):
             bsq_ps[b] = psum.tile([P, Q_TILES, 2], F32, tag="bank", name="bsq_ps")
             for i in range(Q_TILES):
                 nc.tensor.matmul(
@@ -222,24 +214,24 @@ def tile_vidsam_pa_t_kernel(
                 in_=aff_grouped[b][:].rearrange("q p k -> q (p k)"),
             )
 
-        def transpose_values(b):
+        def transpose_values(b, h):
             val_words = val_sb[b][:].bitcast(F32)
-            val_grouped[b] = work.tile([P, C * PACK], BF16, align_bytes=64, name="val_grouped", bufs=2)
+            if h == 0:
+                val_grouped[b] = work.tile([P, C * PACK], BF16, align_bytes=64, name="val_grouped", bufs=2)
             grouped_words = val_grouped[b][:].bitcast(F32)
-            for h in range(2):
-                flipped = psum.tile([P, 2, 2 * P], F32, tag="bank")
-                for tl in range(2):
-                    for u in range(2):
-                        first = (2 * h + tl) * (N // 2)
-                        nc.tensor.transpose(
-                            flipped[:, u, tl * P : (tl + 1) * P],
-                            val_words[:, first + u : first + N // 2 : 2],
-                            ident_f32[:],
-                        )
-                nc.scalar.copy(
-                    out=grouped_words[:, h * N : (h + 1) * N].rearrange("q (c u) -> q c u", u=2),
-                    in_=flipped[:].rearrange("q u c -> q c u"),
-                )
+            flipped = psum.tile([P, 2, 2 * P], F32, tag="bank")
+            for tl in range(2):
+                for u in range(2):
+                    first = (2 * h + tl) * (N // 2)
+                    nc.tensor.transpose(
+                        flipped[:, u, tl * P : (tl + 1) * P],
+                        val_words[:, first + u : first + N // 2 : 2],
+                        ident_f32[:],
+                    )
+            nc.scalar.copy(
+                out=grouped_words[:, h * N : (h + 1) * N].rearrange("q (c u) -> q c u", u=2),
+                in_=flipped[:].rearrange("q u c -> q c u"),
+            )
 
         def quantise_values(b):
             val_codes[b] = work.tile([P, C], U32, align_bytes=64, name="val_codes")
@@ -290,9 +282,16 @@ def tile_vidsam_pa_t_kernel(
             if live(step - 3):
                 group_affinity(step - 3)
             if live(step - 2):
-                transpose_values(step - 2)
+                transpose_values(step - 2, 0)
+            if live(step + 1):
+                distances(step + 1, 0)
+            if live(step - 2):
+                transpose_values(step - 2, 1)
             if live(step - 4):
                 read_memory(step - 4)
+            if live(step + 1):
+                distances(step + 1, 1)
+                query_squares(step + 1)
             if live(step):
                 scale_distances(step, 0)
                 scale_distances(step, 1)
@@ -317,8 +316,6 @@ def tile_vidsam_pa_t_kernel(
             if live(step - 4):
                 copy_result_scalar(step - 4)
                 store_result(step - 4, 0)
-            if live(step + 1):
-                distances(step + 1)
             if live(4 * (step + 1)):
                 spread_shrinkage(4 * (step + 1) + 2)
             if live(step - 2):

@@ -47,7 +47,7 @@ def tile_vidsam_pa_t_kernel(
         ctx.enter_context(tc.manual_schedule())
 
         ms_rows = consts.tile([P, N], BF16)
-        nc.vector.memset(ms_rows[:], 0.0)
+        nc.gpsimd.memset(ms_rows[:].bitcast(F32), 0.0)
         nc.sync.dma_start(out=ms_rows[0:B, :], in_=memory_shrinkage)
         qe_sb, ksq_sb, qs_sb, key_sb, qk_sb, val_sb = {}, {}, {}, {}, {}, {}
 
@@ -78,6 +78,18 @@ def tile_vidsam_pa_t_kernel(
         warm = consts.tile([P, 1], F32)
         nc.scalar.activation(out=warm[:], in_=ones_f32[:, 0:1], func=ACT.Exp)
 
+        qs_m2, prod = {}, {}
+
+        def prepare_queries(b, engine):
+            qs_m2[b] = work.tile([P, Q], BF16, name="qs_m2", bufs=3)
+            engine.tensor_scalar(
+                out=qs_m2[b][:], in0=qs_sb[b][:], scalar1=-2.0, scalar2=0.0, op0=ALU.mult, op1=ALU.add
+            )
+            prod[b] = work.tile([P, Q], F32, name="prod", bufs=3)
+            engine.tensor_tensor(out=prod[b][:], in0=qs_sb[b][:], in1=qk_sb[b][:], op=ALU.mult)
+
+        prepare_queries(0, nc.vector)
+
         ms_words = ms_rows[:].bitcast(F32)
         ms_cols_ps = psum.tile([P, 2, P], F32, tag="bank")
         for k in range(2):
@@ -85,21 +97,12 @@ def tile_vidsam_pa_t_kernel(
         ms_cols = consts.tile([P, 2, B], F32)
         nc.vector.tensor_copy(out=ms_cols[:], in_=ms_cols_ps[:, :, 0:B])
 
-        qs_m2, prod = {}, {}
         shrink = consts.tile([P, B, N], BF16)
         bsq_ps, d_ps, dist, dist_min, neg_max = {}, {}, {}, {}, {}
         expo, expo_sum, inv_sum = {}, {}, {}
         affinity, aff_flipped, aff_grouped, aff_codes, aff_scales = {}, {}, {}, {}, {}
         val_grouped, val_codes, val_scales = {}, {}, {}
         o_ps, result = {}, {}
-
-        def prepare_queries(b):
-            qs_m2[b] = work.tile([P, Q], BF16, name="qs_m2", bufs=3)
-            nc.gpsimd.tensor_scalar(
-                out=qs_m2[b][:], in0=qs_sb[b][:], scalar1=-2.0, scalar2=0.0, op0=ALU.mult, op1=ALU.add
-            )
-            prod[b] = work.tile([P, Q], F32, name="prod", bufs=3)
-            nc.gpsimd.tensor_tensor(out=prod[b][:], in0=qs_sb[b][:], in1=qk_sb[b][:], op=ALU.mult)
 
         def spread_shrinkage(b):
             spread_ps = psum.tile([P, 2, N // 2], F32, tag="bank")
@@ -154,8 +157,8 @@ def tile_vidsam_pa_t_kernel(
 
         def negated_maximum(b):
             neg_max[b] = work.tile([P, Q_TILES], F32, name="neg_max")
-            nc.vector.tensor_scalar(
-                out=neg_max[b][:], in0=dist_min[b][:], scalar1=INV_SQRT_CK, scalar2=None, op0=ALU.mult
+            nc.gpsimd.tensor_scalar(
+                out=neg_max[b][:], in0=dist_min[b][:], scalar1=INV_SQRT_CK, scalar2=0.0, op0=ALU.mult, op1=ALU.add
             )
 
         def exponentials(b):
@@ -178,7 +181,8 @@ def tile_vidsam_pa_t_kernel(
         def normalise(b):
             affinity[b] = work.tile([P, Q_TILES, N], BF16, name="affinity", bufs=2)
             for i in range(Q_TILES):
-                nc.gpsimd.tensor_scalar(
+                engine = nc.vector if b == B - 1 and i == 1 else nc.gpsimd
+                engine.tensor_scalar(
                     out=affinity[b][:, i, :].rearrange("p (u q e) -> p u q e", u=2, e=2),
                     in0=expo[b][:, i, :].rearrange("p (q u e) -> p u q e", u=2, e=2),
                     scalar1=inv_sum[b][:, i : i + 1],
@@ -234,8 +238,8 @@ def tile_vidsam_pa_t_kernel(
             )
 
         def quantise_values(b):
-            val_codes[b] = work.tile([P, C], U32, align_bytes=64, name="val_codes")
-            val_scales[b] = work.tile([P, C], U8, align_bytes=64, name="val_scales")
+            val_codes[b] = work.tile([P, C], U32, align_bytes=64, name="val_codes", bufs=4)
+            val_scales[b] = work.tile([P, C], U8, align_bytes=64, name="val_scales", bufs=4)
             nc.vector.quantize_mx(
                 out=val_codes[b][:].bitcast(FP8X4), scales=val_scales[b][:], in_=val_grouped[b][:]
             )
@@ -273,7 +277,6 @@ def tile_vidsam_pa_t_kernel(
         def live(b):
             return 0 <= b < B
 
-        prepare_queries(0)
         for step in range(-1, B + 4):
             if live(step + LOAD_AHEAD + 1):
                 load(step + LOAD_AHEAD + 1)
@@ -281,17 +284,19 @@ def tile_vidsam_pa_t_kernel(
                 exponentials(step - 1)
             if live(step - 3):
                 group_affinity(step - 3)
-            if live(step - 2):
-                transpose_values(step - 2, 0)
+            if live(step):
+                transpose_values(step, 0)
+            if live(4 * (step + 1)):
+                spread_shrinkage(4 * (step + 1))
             if live(step + 1):
+                query_squares(step + 1)
                 distances(step + 1, 0)
-            if live(step - 2):
-                transpose_values(step - 2, 1)
+            if live(step):
+                transpose_values(step, 1)
             if live(step - 4):
                 read_memory(step - 4)
             if live(step + 1):
                 distances(step + 1, 1)
-                query_squares(step + 1)
             if live(step):
                 scale_distances(step, 0)
                 scale_distances(step, 1)
@@ -300,19 +305,24 @@ def tile_vidsam_pa_t_kernel(
             if live(step - 2):
                 normalise(step - 2)
             if live(step + 2):
-                prepare_queries(step + 2)
-            if live(step - 4):
+                prepare_queries(step + 2, nc.gpsimd)
+            draining = step >= B
+            if live(step - 4) and not draining:
                 copy_result_vector(step - 4)
                 store_result(step - 4, 1)
             if live(step):
                 negated_maximum(step)
-            if live(step - 3):
-                quantise_values(step - 3)
-                quantise_affinity(step - 3)
-            if live(step - 1):
+            if live(step - 1) and draining:
                 invert_sums(step - 1)
-            if live(4 * (step + 1)):
-                spread_shrinkage(4 * (step + 1))
+            if live(step - 1):
+                quantise_values(step - 1)
+            if live(step - 3):
+                quantise_affinity(step - 3)
+            if live(step - 1) and not draining:
+                invert_sums(step - 1)
+            if live(step - 4) and draining:
+                copy_result_vector(step - 4)
+                store_result(step - 4, 1)
             if live(step - 4):
                 copy_result_scalar(step - 4)
                 store_result(step - 4, 0)

@@ -157,8 +157,8 @@ def tile_vidsam_pa_t_kernel(
 
         def negated_maximum(b):
             neg_max[b] = work.tile([P, Q_TILES], F32, name="neg_max")
-            nc.gpsimd.tensor_scalar(
-                out=neg_max[b][:], in0=dist_min[b][:], scalar1=INV_SQRT_CK, scalar2=0.0, op0=ALU.mult, op1=ALU.add
+            nc.vector.tensor_scalar(
+                out=neg_max[b][:], in0=dist_min[b][:], scalar1=INV_SQRT_CK, scalar2=None, op0=ALU.mult
             )
 
         def exponentials(b):

@@ -82,9 +82,7 @@ def tile_vidsam_pa_t_kernel(
 
         def prepare_queries(b, engine):
             qs_m2[b] = work.tile([P, Q], BF16, name="qs_m2", bufs=3)
-            engine.tensor_scalar(
-                out=qs_m2[b][:], in0=qs_sb[b][:], scalar1=-2.0, scalar2=0.0, op0=ALU.mult, op1=ALU.add
-            )
+            nc.scalar.mul(out=qs_m2[b][:], in_=qs_sb[b][:], mul=-2.0)
             prod[b] = work.tile([P, Q], F32, name="prod", bufs=3)
             engine.tensor_tensor(out=prod[b][:], in0=qs_sb[b][:], in1=qk_sb[b][:], op=ALU.mult)
 

@@ -80,13 +80,18 @@ def tile_vidsam_pa_t_kernel(
 
         qs_m2, prod = {}, {}
 
-        def prepare_queries(b, engine):
+        def double_queries(b):
             qs_m2[b] = work.tile([P, Q], BF16, name="qs_m2", bufs=3)
-            nc.scalar.mul(out=qs_m2[b][:], in_=qs_sb[b][:], mul=-2.0)
+            nc.vector.tensor_scalar(
+                out=qs_m2[b][:], in0=qs_sb[b][:], scalar1=-2.0, scalar2=None, op0=ALU.mult
+            )
+
+        def multiply_queries(b, engine):
             prod[b] = work.tile([P, Q], F32, name="prod", bufs=3)
             engine.tensor_tensor(out=prod[b][:], in0=qs_sb[b][:], in1=qk_sb[b][:], op=ALU.mult)
 
-        prepare_queries(0, nc.vector)
+        double_queries(0)
+        multiply_queries(0, nc.vector)
 
         ms_words = ms_rows[:].bitcast(F32)
         ms_cols_ps = psum.tile([P, 2, P], F32, tag="bank")
@@ -111,7 +116,10 @@ def tile_vidsam_pa_t_kernel(
                         ms_cols[:, k, b + j : b + j + 1].to_broadcast([P, P]),
                         ident_f32[:],
                     )
-            nc.scalar.copy(out=shrink[:, b : b + 2, :].bitcast(F32), in_=spread_ps[:])
+            if b == 2:
+                nc.vector.tensor_copy(out=shrink[:, b : b + 2, :].bitcast(F32), in_=spread_ps[:])
+            else:
+                nc.scalar.copy(out=shrink[:, b : b + 2, :].bitcast(F32), in_=spread_ps[:])
 
         def distances(b, i):
             q_cols = slice(i * P, (i + 1) * P)
@@ -258,7 +266,7 @@ def tile_vidsam_pa_t_kernel(
                     )
 
         def copy_result_vector(b):
-            result[b] = work.tile([P, C_TILES * Q], F32, name="result")
+            result[b] = work.tile([P, C_TILES * Q], F32, name="result", bufs=4)
             nc.vector.tensor_copy(
                 out=result[b][:, 2 * Q : 4 * Q], in_=o_ps[b, 1][:].rearrange("r t p -> r (t p)")
             )
@@ -284,8 +292,9 @@ def tile_vidsam_pa_t_kernel(
                 group_affinity(step - 3)
             if live(step):
                 transpose_values(step, 0)
-            if live(4 * (step + 1)):
-                spread_shrinkage(4 * (step + 1))
+            if step == -1:
+                spread_shrinkage(0)
+                spread_shrinkage(2)
             if live(step + 1):
                 query_squares(step + 1)
                 distances(step + 1, 0)
@@ -303,7 +312,7 @@ def tile_vidsam_pa_t_kernel(
             if live(step - 2):
                 normalise(step - 2)
             if live(step + 2):
-                prepare_queries(step + 2, nc.gpsimd)
+                multiply_queries(step + 2, nc.gpsimd)
             draining = step >= B
             if live(step - 4) and not draining:
                 copy_result_vector(step - 4)
@@ -316,6 +325,8 @@ def tile_vidsam_pa_t_kernel(
                 quantise_values(step - 1)
             if live(step - 3):
                 quantise_affinity(step - 3)
+            if live(step + 2):
+                double_queries(step + 2)
             if live(step - 1) and not draining:
                 invert_sums(step - 1)
             if live(step - 4) and draining:
@@ -324,7 +335,7 @@ def tile_vidsam_pa_t_kernel(
             if live(step - 4):
                 copy_result_scalar(step - 4)
                 store_result(step - 4, 0)
-            if live(4 * (step + 1)):
-                spread_shrinkage(4 * (step + 1) + 2)
+            if step >= 0 and live(2 * step + 4):
+                spread_shrinkage(2 * step + 4)
             if live(step - 2):
                 transpose_affinity(step - 2)

import math
from contextlib import ExitStack

import concourse.mybir as mybir
from concourse.masks import make_identity

F32 = mybir.dt.float32
BF16 = mybir.dt.bfloat16
U32 = mybir.dt.uint32
U8 = mybir.dt.uint8
FP8X4 = mybir.dt.float8_e4m3fn_x4
ALU = mybir.AluOpType
ACT = mybir.ActivationFunctionType
AXIS = mybir.AxisListType

P = 128
B = 16
N = 512
Q = 256
C = 512
Q_TILES = Q // P
C_TILES = C // P
PACK = 4
INV_SQRT_CK = 1.0 / math.sqrt(128.0)
LOAD_AHEAD = 4

FLOPS = B * (2 * 2 * P * N * Q + 2 * C * N * Q)


def tile_vidsam_pa_t_kernel(
    tc,
    memory_key,
    memory_key_sq,
    query_key,
    query_selection,
    query_key_sel,
    memory_shrinkage,
    memory_value,
    out,
):
    nc = tc.nc
    with ExitStack() as ctx:
        consts = ctx.enter_context(tc.tile_pool(name="consts", bufs=1))
        loads = ctx.enter_context(tc.tile_pool(name="loads", bufs=B))
        work = ctx.enter_context(tc.tile_pool(name="work", bufs=3))
        psum = ctx.enter_context(tc.psum_pool(name="psum", bufs=8))
        ctx.enter_context(tc.manual_schedule())

        ms_rows = consts.tile([P, N], BF16)
        nc.gpsimd.memset(ms_rows[:].bitcast(F32), 0.0)
        nc.sync.dma_start(out=ms_rows[0:B, :], in_=memory_shrinkage)
        qe_sb, ksq_sb, qs_sb, key_sb, qk_sb, val_sb = {}, {}, {}, {}, {}, {}

        def load(b):
            qs_sb[b] = loads.tile([P, Q], BF16, name="qs")
            nc.sync.dma_start(out=qs_sb[b][:], in_=query_key_sel[b])
            qk_sb[b] = loads.tile([P, Q], BF16, name="qk")
            nc.sync.dma_start(out=qk_sb[b][:], in_=query_key[b])
            qe_sb[b] = loads.tile([P, Q], BF16, name="qe")
            nc.sync.dma_start(out=qe_sb[b][:], in_=query_selection[b])
            ksq_sb[b] = loads.tile([P, N], BF16, name="ksq")
            nc.sync.dma_start(out=ksq_sb[b][:], in_=memory_key_sq[b])
            key_sb[b] = loads.tile([P, N], BF16, name="key")
            nc.sync.dma_start(out=key_sb[b][:], in_=memory_key[b])
            val_sb[b] = loads.tile([P, C_TILES * N], BF16, name="val")
            nc.sync.dma_start(
                out=val_sb[b][:],
                in_=memory_value[b].rearrange("(r t) n -> r (t n)", t=C_TILES),
            )

        for b in range(LOAD_AHEAD):
            load(b)

        ident_f32 = consts.tile([P, P], F32)
        make_identity(nc, ident_f32[:])
        ones_f32 = consts.tile([P, 2], F32)
        nc.vector.memset(ones_f32[:], 1.0)
        warm = consts.tile([P, 1], F32)
        nc.scalar.activation(out=warm[:], in_=ones_f32[:, 0:1], func=ACT.Exp)

        qs_m2, prod = {}, {}

        def double_queries(b):
            qs_m2[b] = work.tile([P, Q], BF16, name="qs_m2", bufs=3)
            nc.vector.tensor_scalar(
                out=qs_m2[b][:], in0=qs_sb[b][:], scalar1=-2.0, scalar2=None, op0=ALU.mult
            )

        def multiply_queries(b, engine):
            prod[b] = work.tile([P, Q], F32, name="prod", bufs=3)
            engine.tensor_tensor(out=prod[b][:], in0=qs_sb[b][:], in1=qk_sb[b][:], op=ALU.mult)

        double_queries(0)
        multiply_queries(0, nc.vector)

        ms_words = ms_rows[:].bitcast(F32)
        ms_cols_ps = psum.tile([P, 2, P], F32, tag="bank")
        for k in range(2):
            nc.tensor.transpose(ms_cols_ps[:, k, :], ms_words[:, k * P : (k + 1) * P], ident_f32[:])
        ms_cols = consts.tile([P, 2, B], F32)
        nc.vector.tensor_copy(out=ms_cols[:], in_=ms_cols_ps[:, :, 0:B])

        shrink = consts.tile([P, B, N], BF16)
        bsq_ps, d_ps, dist, dist_min, neg_max = {}, {}, {}, {}, {}
        expo, expo_sum, inv_sum = {}, {}, {}
        affinity, aff_flipped, aff_grouped, aff_codes, aff_scales = {}, {}, {}, {}, {}
        val_grouped, val_codes, val_scales = {}, {}, {}
        o_ps, result = {}, {}

        def spread_shrinkage(b):
            spread_ps = psum.tile([P, 2, N // 2], F32, tag="bank")
            for j in range(2):
                for k in range(2):
                    nc.tensor.transpose(
                        spread_ps[:, j, k * P : (k + 1) * P],
                        ms_cols[:, k, b + j : b + j + 1].to_broadcast([P, P]),
                        ident_f32[:],
                    )
            if b == 2:
                nc.vector.tensor_copy(out=shrink[:, b : b + 2, :].bitcast(F32), in_=spread_ps[:])
            else:
                nc.scalar.copy(out=shrink[:, b : b + 2, :].bitcast(F32), in_=spread_ps[:])

        def distances(b, i):
            q_cols = slice(i * P, (i + 1) * P)
            d_ps[b, i] = psum.tile([P, N], F32, tag="bank", name="d_ps")
            nc.tensor.matmul(
                out=d_ps[b, i][:], lhsT=qe_sb[b][:, q_cols], rhs=ksq_sb[b][:], start=True, stop=False
            )
            nc.tensor.matmul(
                out=d_ps[b, i][:], lhsT=qs_m2[b][:, q_cols], rhs=key_sb[b][:], start=False, stop=True
            )

        def query_squares(b):
            bsq_ps[b] = psum.tile([P, Q_TILES, 2], F32, tag="bank", name="bsq_ps")
            for i in range(Q_TILES):
                nc.tensor.matmul(
                    out=bsq_ps[b][:, i, :],
                    lhsT=prod[b][:, i * P : (i + 1) * P],
                    rhs=ones_f32[:],
                    start=True,
                    stop=True,
                )

        def scale_distances(b, i):
            if i == 0:
                dist[b] = work.tile([P, Q_TILES, N], F32, name="dist")
            nc.vector.scalar_tensor_tensor(
                out=dist[b][:, i, :],
                in0=d_ps[b, i][:],
                scalar=bsq_ps[b][:, i, 0:1],
                in1=shrink[:, b, :],
                op0=ALU.add,
                op1=ALU.mult,
            )

        def row_minimum(b, i):
            if i == 0:
                dist_min[b] = work.tile([P, Q_TILES], F32, name="dist_min")
            nc.vector.tensor_reduce(
                out=dist_min[b][:, i : i + 1], in_=dist[b][:, i, :], axis=AXIS.X, op=ALU.min
            )

        def negated_maximum(b):
            neg_max[b] = work.tile([P, Q_TILES], F32, name="neg_max")
            nc.vector.tensor_scalar(
                out=neg_max[b][:], in0=dist_min[b][:], scalar1=INV_SQRT_CK, scalar2=None, op0=ALU.mult
            )

        def exponentials(b):
            expo[b] = work.tile([P, Q_TILES, N], F32, name="expo")
            expo_sum[b] = work.tile([P, Q_TILES], F32, name="expo_sum")
            for i in range(Q_TILES):
                nc.scalar.activation(
                    out=expo[b][:, i, :],
                    in_=dist[b][:, i, :],
                    func=ACT.Exp,
                    bias=neg_max[b][:, i : i + 1],
                    scale=-INV_SQRT_CK,
                    accum_out=expo_sum[b][:, i : i + 1],
                )

        def invert_sums(b):
            inv_sum[b] = work.tile([P, Q_TILES], F32, name="inv_sum")
            nc.vector.reciprocal(out=inv_sum[b][:], in_=expo_sum[b][:])

        def normalise(b):
            affinity[b] = work.tile([P, Q_TILES, N], BF16, name="affinity", bufs=2)
            for i in range(Q_TILES):
                engine = nc.vector if b == B - 1 and i == 1 else nc.gpsimd
                engine.tensor_scalar(
                    out=affinity[b][:, i, :].rearrange("p (u q e) -> p u q e", u=2, e=2),
                    in0=expo[b][:, i, :].rearrange("p (q u e) -> p u q e", u=2, e=2),
                    scalar1=inv_sum[b][:, i : i + 1],
                    scalar2=0.0,
                    op0=ALU.mult,
                    op1=ALU.add,
                )

        def transpose_affinity(b):
            aff_flipped[b] = psum.tile([P, 2, Q], F32, tag="bank", name="aff_flipped")
            for i in range(Q_TILES):
                aff_words = affinity[b][:, i, :].bitcast(F32)
                for u in range(2):
                    nc.tensor.transpose(
                        aff_flipped[b][:, u, i * P : (i + 1) * P],
                        aff_words[:, u * P : (u + 1) * P],
                        ident_f32[:],
                    )

        def group_affinity(b):
            aff_grouped[b] = work.tile([P, Q, PACK], BF16, align_bytes=64, name="aff_grouped", bufs=2)
            nc.scalar.copy(
                out=aff_grouped[b][:].bitcast(F32),
                in_=aff_flipped[b][:].rearrange("q u p -> q p u"),
            )

        def quantise_affinity(b):
            aff_codes[b] = work.tile([P, Q], U32, align_bytes=64, name="aff_codes")
            aff_scales[b] = work.tile([P, Q], U8, align_bytes=64, name="aff_scales")
            nc.vector.quantize_mx(
                out=aff_codes[b][:].bitcast(FP8X4),
                scales=aff_scales[b][:],
                in_=aff_grouped[b][:].rearrange("q p k -> q (p k)"),
            )

        def transpose_values(b, h):
            val_words = val_sb[b][:].bitcast(F32)
            if h == 0:
                val_grouped[b] = work.tile([P, C * PACK], BF16, align_bytes=64, name="val_grouped", bufs=2)
            grouped_words = val_grouped[b][:].bitcast(F32)
            flipped = psum.tile([P, 2, 2 * P], F32, tag="bank")
            for tl in range(2):
                for u in range(2):
                    first = (2 * h + tl) * (N // 2)
                    nc.tensor.transpose(
                        flipped[:, u, tl * P : (tl + 1) * P],
                        val_words[:, first + u : first + N // 2 : 2],
                        ident_f32[:],
                    )
            nc.scalar.copy(
                out=grouped_words[:, h * N : (h + 1) * N].rearrange("q (c u) -> q c u", u=2),
                in_=flipped[:].rearrange("q u c -> q c u"),
            )

        def quantise_values(b):
            val_codes[b] = work.tile([P, C], U32, align_bytes=64, name="val_codes", bufs=4)
            val_scales[b] = work.tile([P, C], U8, align_bytes=64, name="val_scales", bufs=4)
            nc.vector.quantize_mx(
                out=val_codes[b][:].bitcast(FP8X4), scales=val_scales[b][:], in_=val_grouped[b][:]
            )

        def read_memory(b):
            for h in range(2):
                o_ps[b, h] = psum.tile([P, 2, Q], F32, tag="bank", name="o_ps")
                for tl in range(2):
                    c_cols = slice((2 * h + tl) * P, (2 * h + tl + 1) * P)
                    nc.tensor.matmul_mx(
                        out=o_ps[b, h][:, tl, :],
                        lhsT=val_codes[b][:, c_cols].bitcast(FP8X4),
                        lhsT_scale=val_scales[b][:, c_cols],
                        rhs=aff_codes[b][:].bitcast(FP8X4),
                        rhs_scale=aff_scales[b][:],
                        start=True,
                        stop=True,
                    )

        def copy_result_vector(b):
            result[b] = work.tile([P, C_TILES * Q], F32, name="result", bufs=4)
            nc.vector.tensor_copy(
                out=result[b][:, 2 * Q : 4 * Q], in_=o_ps[b, 1][:].rearrange("r t p -> r (t p)")
            )

        def copy_result_scalar(b):
            nc.scalar.copy(out=result[b][:, 0 : 2 * Q], in_=o_ps[b, 0][:].rearrange("r t p -> r (t p)"))

        def store_result(b, h):
            half = slice(h * 2 * Q, (h + 1) * 2 * Q)
            nc.sync.dma_start(
                out=out[b].rearrange("(r t) p -> r (t p)", t=C_TILES)[:, half], in_=result[b][:, half]
            )

        def live(b):
            return 0 <= b < B

        for step in range(-1, B + 4):
            if live(step + LOAD_AHEAD + 1):
                load(step + LOAD_AHEAD + 1)
            if live(step - 1):
                exponentials(step - 1)
            if live(step - 3):
                group_affinity(step - 3)
            if live(step):
                transpose_values(step, 0)
            if step == -1:
                spread_shrinkage(0)
                spread_shrinkage(2)
            if live(step + 1):
                query_squares(step + 1)
                distances(step + 1, 0)
            if live(step):
                transpose_values(step, 1)
            if live(step - 4):
                read_memory(step - 4)
            if live(step + 1):
                distances(step + 1, 1)
            if live(step):
                scale_distances(step, 0)
                scale_distances(step, 1)
                row_minimum(step, 0)
                row_minimum(step, 1)
            if live(step - 2):
                normalise(step - 2)
            if live(step + 2):
                multiply_queries(step + 2, nc.gpsimd)
            draining = step >= B
            if live(step - 4) and not draining:
                copy_result_vector(step - 4)
                store_result(step - 4, 1)
            if live(step):
                negated_maximum(step)
            if live(step - 1) and draining:
                invert_sums(step - 1)
            if live(step - 1):
                quantise_values(step - 1)
            if live(step - 3):
                quantise_affinity(step - 3)
            if live(step + 2):
                double_queries(step + 2)
            if live(step - 1) and not draining:
                invert_sums(step - 1)
            if live(step - 4) and draining:
                copy_result_vector(step - 4)
                store_result(step - 4, 1)
            if live(step - 4):
                copy_result_scalar(step - 4)
                store_result(step - 4, 0)
            if step >= 0 and live(2 * step + 4):
                spread_shrinkage(2 * step + 4)
            if live(step - 2):
                transpose_affinity(step - 2)
